import numpy as np
import ml_dtypes


def mxq(x, axis, fmt="e4m3"):
    dtype, down = {"e4m3": (ml_dtypes.float8_e4m3fn, 7), "e5m2": (ml_dtypes.float8_e5m2, 14)}[fmt]
    v = np.moveaxis(np.asarray(x, np.float32).astype(ml_dtypes.bfloat16).astype(np.float64), axis, -1)
    blocks = v.reshape(v.shape[:-1] + (-1, 32))
    amax = np.abs(blocks).max(-1, keepdims=True)
    byte = np.maximum(np.where(amax > 0, np.frexp(amax)[1] - 1 + 127, 0) - down, 1)
    scale = np.exp2(byte - 127.0)
    codes = (blocks / scale).astype(np.float32).astype(dtype).astype(np.float64)
    return np.moveaxis((codes * scale).reshape(v.shape), -1, axis)


WIDE = False


def mx_kscale(k):
    if not WIDE:
        return np.ones(k)
    levels = np.array([10, -10, 5, -5, 0])
    a = np.random.permutation(np.resize(levels, k // 512 * 4)).reshape(k // 512, 4)
    idx = np.arange(k)
    return np.exp2(a[idx // 512, idx % 128 // 32])


BF16 = ml_dtypes.bfloat16


def bf(x):
    return np.asarray(x, np.float32).astype(BF16)


def f64(x):
    return np.asarray(x).astype(np.float64)


B, IN, HID, N, NM = 8, 384, 128, 512, 5
C = IN + HID
K = NM * C


def setup_inputs():
    t = mx_kscale(C)
    tc = t[None, :, None]
    return {"x_cand": bf(np.random.standard_normal((B, C, N)) * 0.8 * tc),
            "x1_0": bf(np.random.standard_normal((B, C, N)) * 0.55 * tc),
            "x1_1": bf(np.random.standard_normal((B, C, N)) * 0.55 * tc),
            "support0": bf(np.random.standard_normal((N, N)) * 0.7 / np.sqrt(N)),
            "support1": bf(np.random.standard_normal((N, N)) * 0.7 / np.sqrt(N)),
            "W_c": bf(np.random.standard_normal((K, HID)) / np.sqrt(K) / np.tile(t, NM)[:, None]),
            "b_c": bf(0.3 * np.random.standard_normal(HID)),
            "u": bf(1.0 / (1.0 + np.exp(-(1.0 + np.random.standard_normal((B, HID, N)))))),
            "hx": bf(np.random.standard_normal((B, HID, N)))}


def reference(x_cand, x1_0, x1_1, support0, support1, W_c, b_c, u, hx):
    x0, xa, xb = f64(x_cand), f64(x1_0), f64(x1_1)
    x2a = 2.0 * (mxq(xa, 2, "e4m3") @ mxq(f64(support0).T, 0, "e4m3")) - x0
    x2b = 2.0 * (mxq(xb, 2, "e4m3") @ mxq(f64(support1).T, 0, "e4m3")) - x0
    h = np.concatenate([x0, xa, x2a, xb, x2b], axis=1)
    cand = np.tanh((mxq(f64(W_c).T, 1, "e4m3") @ mxq(h, 1, "e4m3")) + f64(b_c)[None, :, None])
    return f64(u) * f64(hx) + (1.0 - f64(u)) * cand

@@ -1,0 +1,241 @@
+from contextlib import ExitStack
+
+import concourse.mybir as mybir
+from concourse.masks import make_identity
+
+F32 = mybir.dt.float32
+BF16 = mybir.dt.bfloat16
+U32 = mybir.dt.uint32
+U8 = mybir.dt.uint8
+FP8X4 = mybir.dt.float8_e4m3fn_x4
+ALU = mybir.AluOpType
+ACT = mybir.ActivationFunctionType
+
+P = 128
+PACK = 4
+BATCH = 8
+CH = 512
+NODES = 512
+HID = 128
+W_TILE = PACK * NODES
+FLOPS = 2 * (2 * BATCH * CH * NODES * NODES) + 2 * BATCH * HID * 5 * CH * NODES
+
+MANUAL = False
+LOOKAHEAD = 4
+W_BLOCK = (0, 1, 3, 2, 4)
+
+
+def tile_dcgrucell_pc_t_kernel(tc, x_cand, x1_0, x1_1, support0, support1, W_c, b_c, u, hx, out):
+    nc = tc.nc
+    with ExitStack() as ctx:
+        if MANUAL:
+            ctx.enter_context(tc.manual_schedule())
+        const = ctx.enter_context(tc.tile_pool(name="const", bufs=1))
+        xin = ctx.enter_context(tc.tile_pool(name="xin", bufs=16))
+        work = ctx.enter_context(tc.tile_pool(name="work", bufs=2))
+        ps_t = ctx.enter_context(tc.psum_pool(name="ps_t", bufs=2))
+        ps_x = ctx.enter_context(tc.psum_pool(name="ps_x", bufs=4))
+        ps_o = ctx.enter_context(tc.psum_pool(name="ps_o", bufs=2))
+
+        ident = const.tile([P, P], F32, name="ident")
+        make_identity(nc, ident[:])
+
+        raw = {}
+
+        def load_x(key, src):
+            t = xin.tile([P, W_TILE], BF16, name="xin", tag="xin")
+            nc.sync.dma_start(out=t[:], in_=src.rearrange("(p j) n -> p (j n)", j=PACK))
+            raw[key] = t
+
+        def load_support(key, src):
+            t = xin.tile([P, W_TILE], BF16, name="xin", tag="xin")
+            nc.sync.dma_start(
+                out=t[:].rearrange("p (t n) -> p t n", t=PACK),
+                in_=src.rearrange("(t p) n -> p t n", p=P),
+            )
+            raw[key] = t
+
+        def load_batch(b):
+            load_x(("a", b), x1_0[b])
+            load_x(("0", b), x_cand[b])
+            load_x(("b", b), x1_1[b])
+
+        load_x(("a", 0), x1_0[0])
+        load_support("s0", support0)
+        load_x(("0", 0), x_cand[0])
+        load_x(("b", 0), x1_1[0])
+        load_support("s1", support1)
+        w_raw = const.tile([P, 5, PACK, HID], BF16, name="w_raw")
+        nc.sync.dma_start(out=w_raw[:], in_=W_c.rearrange("(g p j) o -> p g j o", p=P, j=PACK))
+        bias_bf = const.tile([P, 1], BF16, name="bias_bf")
+        with nc.allow_non_contiguous_dma(reason="one bias value a partition"):
+            nc.sync.dma_start(out=bias_bf[:], in_=b_c.rearrange("(p o) -> p o", o=1))
+        load_batch(1)
+        u_sb = const.tile([P, BATCH, NODES], BF16, name="u_sb")
+        nc.sync.dma_start(out=u_sb[:], in_=u.rearrange("b o n -> o b n"))
+        hx_sb = const.tile([P, BATCH, NODES], BF16, name="hx_sb")
+        nc.sync.dma_start(out=hx_sb[:], in_=hx.rearrange("b o n -> o b n"))
+        for b in range(2, LOOKAHEAD):
+            load_batch(b)
+
+        def transpose_words(src, dst):
+            srcw = src[:].bitcast(F32)
+            dstw = dst[:].bitcast(F32)
+            for h in range(2):
+                pt = ps_t.tile([P, 2, 256], F32, name="pt", tag="pt")
+                for jj in range(2):
+                    for uu in range(2):
+                        col = (2 * h + jj) * 256 + uu * P
+                        nc.tensor.transpose(pt[:, uu, jj * P : (jj + 1) * P], srcw[:, col : col + P], ident[:])
+                nc.scalar.copy(
+                    out=dstw[:, h * 512 : (h + 1) * 512].rearrange("p (c u) -> p c u", u=2),
+                    in_=pt[:].rearrange("p u c -> p c u"),
+                )
+
+        def quantise(src, codes, scales):
+            nc.vector.quantize_mx(out=codes.bitcast(FP8X4), scales=scales, in_=src)
+
+        def regroup(engine_copy, src, dst):
+            engine_copy(
+                out=dst.rearrange("p (c i t) -> p c t i", i=4, t=PACK),
+                in_=src.rearrange("p (t c i) -> p c t i", t=PACK, i=4),
+            )
+
+        g1 = {}
+        c1 = {}
+
+        def flip(s, b):
+            g = work.tile([P, W_TILE], BF16, name="g1" + s, tag="g1" + s, align_bytes=64)
+            transpose_words(raw[(s, b)], g)
+            g1[(s, b)] = g
+
+        def quantise_flipped(s, b):
+            codes = work.tile([P, NODES], U32, name="c1" + s, tag="c1" + s, align_bytes=64)
+            scales = work.tile([P, NODES], U8, name="s1" + s, tag="s1" + s, align_bytes=64)
+            quantise(g1[(s, b)][:], codes[:], scales[:])
+            c1[(s, b)] = (codes, scales)
+
+        sup = {}
+
+        def prepare_support(key):
+            g = work.tile([P, W_TILE], BF16, name="gs", tag="gs", align_bytes=64)
+            transpose_words(raw[key], g)
+            codes = const.tile([P, NODES], U32, name="c" + key, align_bytes=64)
+            scales = const.tile([P, NODES], U8, name="p" + key, align_bytes=64)
+            quantise(g[:], codes[:], scales[:])
+            sup[key] = (codes, scales)
+
+        hg = {}
+        x2g = {}
+        hq = {}
+
+        def regroup_batch(b, copies):
+            g = work.tile([P, 3, W_TILE], BF16, name="hg", tag="hg", align_bytes=64)
+            hg[b] = g
+            for k, s in enumerate(("0", "a", "b")):
+                regroup(copies[k], raw[(s, b)][:], g[:, k, :])
+
+        def quantise_inputs(b):
+            codes = work.tile([P, 5, NODES], U32, name="hc", tag="hc", align_bytes=64)
+            scales = work.tile([P, 5, NODES], U8, name="hs", tag="hs", align_bytes=64)
+            hq[b] = (codes, scales)
+            for k in range(3):
+                quantise(hg[b][:, k, :], codes[:, k, :], scales[:, k, :])
+
+        def diffuse(s, b):
+            si = 0 if s == "a" else 1
+            if si == 0:
+                x2 = work.tile([P, 2, W_TILE], BF16, name="x2g", tag="x2g", align_bytes=64)
+                x2g[b] = x2
+            codes, scales = c1[(s, b)]
+            scodes, sscales = sup["s%d" % si]
+            for mq in range(4):
+                px = ps_x.tile([P, PACK, P], F32, name="px", tag="px")
+                mcols = slice(mq * P, (mq + 1) * P)
+                for j in range(PACK):
+                    ccols = slice(j * P, (j + 1) * P)
+                    nc.tensor.matmul_mx(
+                        out=px[:, j, :],
+                        lhsT=codes[:, ccols].bitcast(FP8X4),
+                        lhsT_scale=scales[:, ccols],
+                        rhs=scodes[:, mcols].bitcast(FP8X4),
+                        rhs_scale=sscales[:, mcols],
+                        start=True,
+                        stop=True,
+                    )
+                gcols = slice(mq * 512, (mq + 1) * 512)
+                nc.vector.scalar_tensor_tensor(
+                    out=x2g[b][:, si, gcols].rearrange("p (m j) -> p m j", j=PACK),
+                    in0=px[:].rearrange("p j m -> p m j"),
+                    scalar=2.0,
+                    in1=hg[b][:, 0, gcols].rearrange("p (m j) -> p m j", j=PACK),
+                    op0=ALU.mult,
+                    op1=ALU.subtract,
+                )
+
+        def quantise_x2(s, b):
+            si = 0 if s == "a" else 1
+            codes, scales = hq[b]
+            quantise(x2g[b][:, si, :], codes[:, 3 + si, :], scales[:, 3 + si, :])
+
+        def mix(b):
+            codes, scales = hq[b]
+            po = ps_o.tile([P, NODES], F32, name="po", tag="po")
+            for k in range(5):
+                wcols = slice(W_BLOCK[k] * HID, (W_BLOCK[k] + 1) * HID)
+                nc.tensor.matmul_mx(
+                    out=po[:],
+                    lhsT=w_codes[:, wcols].bitcast(FP8X4),
+                    lhsT_scale=w_scales[:, wcols],
+                    rhs=codes[:, k, :].bitcast(FP8X4),
+                    rhs_scale=scales[:, k, :],
+                    start=(k == 0),
+                    stop=(k == 4),
+                )
+            cand = work.tile([P, NODES], F32, name="cand", tag="cand")
+            nc.scalar.activation(out=cand[:], in_=po[:], func=ACT.Tanh, bias=bias[:, 0:1], scale=1.0)
+            res = work.tile([P, NODES], F32, name="res", tag="res")
+            eng = nc.vector if b == BATCH - 1 else nc.gpsimd
+            eng.tensor_tensor(out=res[:], in0=hx_sb[:, b, :], in1=cand[:], op=ALU.subtract)
+            eng.tensor_tensor(out=res[:], in0=res[:], in1=u_sb[:, b, :], op=ALU.mult)
+            eng.tensor_tensor(out=res[:], in0=res[:], in1=cand[:], op=ALU.add)
+            nc.sync.dma_start(out=out[b], in_=res[:])
+
+        flip("a", 0)
+        prepare_support("s0")
+        quantise_flipped("a", 0)
+        flip("b", 0)
+        prepare_support("s1")
+        quantise_flipped("b", 0)
+        w_grp = const.tile([P, 5, HID, PACK], BF16, name="w_grp", align_bytes=64)
+        nc.vector.tensor_copy(out=w_grp[:], in_=w_raw[:].rearrange("p g j o -> p g o j"))
+        bias = const.tile([P, 1], F32, name="bias")
+        nc.vector.tensor_copy(out=bias[:], in_=bias_bf[:])
+        regroup_batch(0, (nc.vector.tensor_copy, nc.vector.tensor_copy, nc.vector.tensor_copy))
+        w_codes = const.tile([P, 5 * HID], U32, name="w_codes", align_bytes=64)
+        w_scales = const.tile([P, 5 * HID], U8, name="w_scales", align_bytes=64)
+        w_flat = w_grp[:].rearrange("p g o j -> p (g o j)")
+        quantise(w_flat[:, 0:2048], w_codes[:, 0:512], w_scales[:, 0:512])
+        quantise(w_flat[:, 2048:2560], w_codes[:, 512:640], w_scales[:, 512:640])
+        quantise_inputs(0)
+
+        for i in range(BATCH):
+            nxt = i + 1
+            if i + LOOKAHEAD < BATCH:
+                load_batch(i + LOOKAHEAD)
+            if nxt < BATCH:
+                flip("a", nxt)
+            diffuse("a", i)
+            if nxt < BATCH:
+                quantise_flipped("a", nxt)
+            quantise_x2("a", i)
+            if nxt < BATCH:
+                flip("b", nxt)
+            diffuse("b", i)
+            if nxt < BATCH:
+                quantise_flipped("b", nxt)
+            quantise_x2("b", i)
+            if nxt < BATCH:
+                regroup_batch(nxt, (nc.scalar.copy, nc.scalar.copy, nc.scalar.copy))
+                quantise_inputs(nxt)
+            mix(i)

@@ -20,8 +20,7 @@ HID = 128
 W_TILE = PACK * NODES
 FLOPS = 2 * (2 * BATCH * CH * NODES * NODES) + 2 * BATCH * HID * 5 * CH * NODES
 
-MANUAL = False
-LOOKAHEAD = 4
+MANUAL = True
 W_BLOCK = (0, 1, 3, 2, 4)
 
 
@@ -31,11 +30,12 @@ def tile_dcgrucell_pc_t_kernel(tc, x_cand, x1_0, x1_1, support0, support1, W_c, 
         if MANUAL:
             ctx.enter_context(tc.manual_schedule())
         const = ctx.enter_context(tc.tile_pool(name="const", bufs=1))
-        xin = ctx.enter_context(tc.tile_pool(name="xin", bufs=16))
-        work = ctx.enter_context(tc.tile_pool(name="work", bufs=2))
-        ps_t = ctx.enter_context(tc.psum_pool(name="ps_t", bufs=2))
-        ps_x = ctx.enter_context(tc.psum_pool(name="ps_x", bufs=4))
-        ps_o = ctx.enter_context(tc.psum_pool(name="ps_o", bufs=2))
+        xin = ctx.enter_context(tc.tile_pool(name="xin", bufs=14))
+        two = ctx.enter_context(tc.tile_pool(name="two", bufs=2))
+        three = ctx.enter_context(tc.tile_pool(name="three", bufs=3))
+        ps_t = ctx.enter_context(tc.psum_pool(name="ps_t", bufs=4))
+        ps_x = ctx.enter_context(tc.psum_pool(name="ps_x", bufs=3))
+        ps_o = ctx.enter_context(tc.psum_pool(name="ps_o", bufs=1))
 
         ident = const.tile([P, P], F32, name="ident")
         make_identity(nc, ident[:])
@@ -71,16 +71,15 @@ def tile_dcgrucell_pc_t_kernel(tc, x_cand, x1_0, x1_1, support0, support1, W_c, 
         with nc.allow_non_contiguous_dma(reason="one bias value a partition"):
             nc.sync.dma_start(out=bias_bf[:], in_=b_c.rearrange("(p o) -> p o", o=1))
         load_batch(1)
+        load_batch(2)
         u_sb = const.tile([P, BATCH, NODES], BF16, name="u_sb")
         nc.sync.dma_start(out=u_sb[:], in_=u.rearrange("b o n -> o b n"))
         hx_sb = const.tile([P, BATCH, NODES], BF16, name="hx_sb")
         nc.sync.dma_start(out=hx_sb[:], in_=hx.rearrange("b o n -> o b n"))
-        for b in range(2, LOOKAHEAD):
-            load_batch(b)
+        load_batch(3)
 
-        def transpose_words(src, dst):
+        def transpose_words(src, dstw):
             srcw = src[:].bitcast(F32)
-            dstw = dst[:].bitcast(F32)
             for h in range(2):
                 pt = ps_t.tile([P, 2, 256], F32, name="pt", tag="pt")
                 for jj in range(2):
@@ -95,92 +94,140 @@ def tile_dcgrucell_pc_t_kernel(tc, x_cand, x1_0, x1_1, support0, support1, W_c, 
         def quantise(src, codes, scales):
             nc.vector.quantize_mx(out=codes.bitcast(FP8X4), scales=scales, in_=src)
 
-        def regroup(engine_copy, src, dst):
-            engine_copy(
-                out=dst.rearrange("p (c i t) -> p c t i", i=4, t=PACK),
-                in_=src.rearrange("p (t c i) -> p c t i", t=PACK, i=4),
+        def gp_copy(out, in_):
+            nc.gpsimd.tensor_scalar(out=out, in0=in_, scalar1=1.0, scalar2=0.0, op0=ALU.mult, op1=ALU.add)
+
+        def regroup(copy_fn, src3, dst3):
+            copy_fn(
+                out=dst3.rearrange("p (c i) t -> p c t i", i=4),
+                in_=src3.rearrange("p t (c i) -> p c t i", i=4),
             )
 
         g1 = {}
         c1 = {}
+        SIDE = {"a": 0, "b": 1}
 
         def flip(s, b):
-            g = work.tile([P, W_TILE], BF16, name="g1" + s, tag="g1" + s, align_bytes=64)
-            transpose_words(raw[(s, b)], g)
-            g1[(s, b)] = g
+            if s == "a":
+                g = two.tile([P, 2, W_TILE], BF16, name="g1", tag="g1", align_bytes=64)
+                g1[b] = g
+            transpose_words(raw[(s, b)], g1[b][:, SIDE[s], :].bitcast(F32))
 
-        def quantise_flipped(s, b):
-            codes = work.tile([P, NODES], U32, name="c1" + s, tag="c1" + s, align_bytes=64)
-            scales = work.tile([P, NODES], U8, name="s1" + s, tag="s1" + s, align_bytes=64)
-            quantise(g1[(s, b)][:], codes[:], scales[:])
-            c1[(s, b)] = (codes, scales)
+        def alloc_c1(b):
+            codes = two.tile([P, 2 * NODES], U32, name="c1", tag="c1", align_bytes=64)
+            scales = two.tile([P, 2 * NODES], U8, name="s1", tag="s1", align_bytes=64)
+            c1[b] = (codes, scales)
+
+        def quantise_flipped_half(s, b):
+            codes, scales = c1[b]
+            cols = slice(SIDE[s] * NODES, (SIDE[s] + 1) * NODES)
+            quantise(g1[b][:, SIDE[s], :], codes[:, cols], scales[:, cols])
+
+        def quantise_flipped(b):
+            alloc_c1(b)
+            codes, scales = c1[b]
+            quantise(g1[b][:].rearrange("p a k -> p (a k)"), codes[:], scales[:])
 
         sup = {}
+        sup_g = {}
 
-        def prepare_support(key):
-            g = work.tile([P, W_TILE], BF16, name="gs", tag="gs", align_bytes=64)
-            transpose_words(raw[key], g)
+        def flip_support(key):
+            g = two.tile([P, W_TILE], BF16, name="gs", tag="gs", align_bytes=64)
+            transpose_words(raw[key], g[:].bitcast(F32))
+            sup_g[key] = g
+
+        def quantise_support(key):
             codes = const.tile([P, NODES], U32, name="c" + key, align_bytes=64)
             scales = const.tile([P, NODES], U8, name="p" + key, align_bytes=64)
-            quantise(g[:], codes[:], scales[:])
+            quantise(sup_g[key][:], codes[:], scales[:])
             sup[key] = (codes, scales)
 
         hg = {}
         x2g = {}
         hq = {}
+        SLOT = {"0": 0, "a": 1, "b": 2}
 
-        def regroup_batch(b, copies):
-            g = work.tile([P, 3, W_TILE], BF16, name="hg", tag="hg", align_bytes=64)
-            hg[b] = g
-            for k, s in enumerate(("0", "a", "b")):
-                regroup(copies[k], raw[(s, b)][:], g[:, k, :])
+        def regroup_x(copy_fn, s, b, n0=0, n1=NODES):
+            if b not in hg:
+                g = three.tile([P, 3, W_TILE], BF16, name="hg", tag="hg", align_bytes=64)
+                hg[b] = g
+            regroup(
+                copy_fn,
+                raw[(s, b)][:].rearrange("p (t n) -> p t n", t=PACK)[:, :, n0:n1],
+                hg[b][:, SLOT[s], PACK * n0 : PACK * n1].rearrange("p (n t) -> p n t", t=PACK),
+            )
+
+        def regroup_x_pieces(copy_fn, s, b, first, last):
+            for q in range(first, last):
+                regroup_x(copy_fn, s, b, q * P, (q + 1) * P)
 
         def quantise_inputs(b):
-            codes = work.tile([P, 5, NODES], U32, name="hc", tag="hc", align_bytes=64)
-            scales = work.tile([P, 5, NODES], U8, name="hs", tag="hs", align_bytes=64)
+            codes = two.tile([P, 5, NODES], U32, name="hc", tag="hc", align_bytes=64)
+            scales = two.tile([P, 5, NODES], U8, name="hs", tag="hs", align_bytes=64)
             hq[b] = (codes, scales)
-            for k in range(3):
-                quantise(hg[b][:, k, :], codes[:, k, :], scales[:, k, :])
+            quantise(
+                hg[b][:, 0:2, :].rearrange("p a k -> p (a k)"),
+                codes[:, 0:2, :].rearrange("p a k -> p (a k)"),
+                scales[:, 0:2, :].rearrange("p a k -> p (a k)"),
+            )
+            quantise(hg[b][:, 2, :], codes[:, 2, :], scales[:, 2, :])
 
-        def diffuse(s, b):
-            si = 0 if s == "a" else 1
-            if si == 0:
-                x2 = work.tile([P, 2, W_TILE], BF16, name="x2g", tag="x2g", align_bytes=64)
-                x2g[b] = x2
-            codes, scales = c1[(s, b)]
+        px_of = {}
+
+        def unit(b, k):
+            si = k // 4
+            mq = k % 4
+            codes, scales = c1[b]
             scodes, sscales = sup["s%d" % si]
-            for mq in range(4):
-                px = ps_x.tile([P, PACK, P], F32, name="px", tag="px")
-                mcols = slice(mq * P, (mq + 1) * P)
-                for j in range(PACK):
-                    ccols = slice(j * P, (j + 1) * P)
-                    nc.tensor.matmul_mx(
-                        out=px[:, j, :],
-                        lhsT=codes[:, ccols].bitcast(FP8X4),
-                        lhsT_scale=scales[:, ccols],
-                        rhs=scodes[:, mcols].bitcast(FP8X4),
-                        rhs_scale=sscales[:, mcols],
-                        start=True,
-                        stop=True,
-                    )
-                gcols = slice(mq * 512, (mq + 1) * 512)
-                nc.vector.scalar_tensor_tensor(
-                    out=x2g[b][:, si, gcols].rearrange("p (m j) -> p m j", j=PACK),
-                    in0=px[:].rearrange("p j m -> p m j"),
-                    scalar=2.0,
-                    in1=hg[b][:, 0, gcols].rearrange("p (m j) -> p m j", j=PACK),
-                    op0=ALU.mult,
-                    op1=ALU.subtract,
+            px = ps_x.tile([P, PACK, P], F32, name="px", tag="px")
+            px_of[(b, k)] = px
+            mcols = slice(mq * P, (mq + 1) * P)
+            for j in range(PACK):
+                ccols = slice(si * NODES + j * P, si * NODES + (j + 1) * P)
+                nc.tensor.matmul_mx(
+                    out=px[:, j, :],
+                    lhsT=codes[:, ccols].bitcast(FP8X4),
+                    lhsT_scale=scales[:, ccols],
+                    rhs=scodes[:, mcols].bitcast(FP8X4),
+                    rhs_scale=sscales[:, mcols],
+                    start=True,
+                    stop=True,
                 )
 
-        def quantise_x2(s, b):
-            si = 0 if s == "a" else 1
+        def combine(b, k):
+            si = k // 4
+            mq = k % 4
+            if k == 0:
+                x2 = two.tile([P, 2, W_TILE], BF16, name="x2g", tag="x2g", align_bytes=64)
+                x2g[b] = x2
+            gcols = slice(mq * 512, (mq + 1) * 512)
+            nc.vector.scalar_tensor_tensor(
+                out=x2g[b][:, si, gcols].rearrange("p (m j) -> p m j", j=PACK),
+                in0=px_of[(b, k)][:].rearrange("p j m -> p m j"),
+                scalar=2.0,
+                in1=hg[b][:, 0, gcols].rearrange("p (m j) -> p m j", j=PACK),
+                op0=ALU.mult,
+                op1=ALU.subtract,
+            )
+
+        def quantise_x2(b):
+            codes, scales = hq[b]
+            quantise(
+                x2g[b][:].rearrange("p a k -> p (a k)"),
+                codes[:, 3:5, :].rearrange("p a k -> p (a k)"),
+                scales[:, 3:5, :].rearrange("p a k -> p (a k)"),
+            )
+
+        def quantise_x2_half(b, si):
             codes, scales = hq[b]
             quantise(x2g[b][:, si, :], codes[:, 3 + si, :], scales[:, 3 + si, :])
+
+        po_of = {}
 
         def mix(b):
             codes, scales = hq[b]
             po = ps_o.tile([P, NODES], F32, name="po", tag="po")
+            po_of[b] = po
             for k in range(5):
                 wcols = slice(W_BLOCK[k] * HID, (W_BLOCK[k] + 1) * HID)
                 nc.tensor.matmul_mx(
@@ -192,50 +239,101 @@ def tile_dcgrucell_pc_t_kernel(tc, x_cand, x1_0, x1_1, support0, support1, W_c, 
                     start=(k == 0),
                     stop=(k == 4),
                 )
-            cand = work.tile([P, NODES], F32, name="cand", tag="cand")
-            nc.scalar.activation(out=cand[:], in_=po[:], func=ACT.Tanh, bias=bias[:, 0:1], scale=1.0)
-            res = work.tile([P, NODES], F32, name="res", tag="res")
-            eng = nc.vector if b == BATCH - 1 else nc.gpsimd
+
+        def finish(b, eng):
+            cand = three.tile([P, NODES], F32, name="cand", tag="cand")
+            nc.scalar.activation(out=cand[:], in_=po_of[b][:], func=ACT.Tanh, bias=bias[:, 0:1], scale=1.0)
+            res = three.tile([P, NODES], F32, name="res", tag="res")
             eng.tensor_tensor(out=res[:], in0=hx_sb[:, b, :], in1=cand[:], op=ALU.subtract)
             eng.tensor_tensor(out=res[:], in0=res[:], in1=u_sb[:, b, :], op=ALU.mult)
             eng.tensor_tensor(out=res[:], in0=res[:], in1=cand[:], op=ALU.add)
             nc.sync.dma_start(out=out[b], in_=res[:])
 
+        def flip_both(k):
+            flip("a", k)
+            flip("b", k)
+
+        def diffuse_rest(i):
+            for k in range(8):
+                combine(i, k)
+                if k + 3 < 8:
+                    unit(i, k + 3)
+                if i == BATCH - 1 and k == 5:
+                    quantise_x2_half(i, 0)
+
         flip("a", 0)
-        prepare_support("s0")
-        quantise_flipped("a", 0)
+        flip_support("s0")
+        regroup_x(nc.vector.tensor_copy, "a", 0)
+        alloc_c1(0)
+        quantise_flipped_half("a", 0)
+        regroup_x(nc.vector.tensor_copy, "0", 0)
+        quantise_support("s0")
         flip("b", 0)
-        prepare_support("s1")
-        quantise_flipped("b", 0)
+        flip_support("s1")
+        for k in range(3):
+            unit(0, k)
+        regroup_x(nc.vector.tensor_copy, "b", 0)
         w_grp = const.tile([P, 5, HID, PACK], BF16, name="w_grp", align_bytes=64)
-        nc.vector.tensor_copy(out=w_grp[:], in_=w_raw[:].rearrange("p g j o -> p g o j"))
+        for g in range(5):
+            regroup(gp_copy, w_raw[:, g, :, :], w_grp[:, g, :, :])
+        combine(0, 0)
+        unit(0, 3)
+        for k in range(1, 4):
+            combine(0, k)
+        quantise_flipped_half("b", 0)
+        quantise_support("s1")
         bias = const.tile([P, 1], F32, name="bias")
         nc.vector.tensor_copy(out=bias[:], in_=bias_bf[:])
-        regroup_batch(0, (nc.vector.tensor_copy, nc.vector.tensor_copy, nc.vector.tensor_copy))
+        flip("a", 1)
+        regroup_x(nc.scalar.copy, "0", 1)
+        for k in range(4, 7):
+            unit(0, k)
+        flip("b", 1)
+        regroup_x(nc.scalar.copy, "a", 1)
+        regroup_x(nc.scalar.copy, "b", 1)
+        quantise_inputs(0)
+        combine(0, 4)
+        unit(0, 7)
+        for k in range(5, 8):
+            combine(0, k)
+        load_batch(4)
+        flip_both(2)
+        regroup_x(nc.scalar.copy, "0", 2)
         w_codes = const.tile([P, 5 * HID], U32, name="w_codes", align_bytes=64)
         w_scales = const.tile([P, 5 * HID], U8, name="w_scales", align_bytes=64)
         w_flat = w_grp[:].rearrange("p g o j -> p (g o j)")
         quantise(w_flat[:, 0:2048], w_codes[:, 0:512], w_scales[:, 0:512])
         quantise(w_flat[:, 2048:2560], w_codes[:, 512:640], w_scales[:, 512:640])
-        quantise_inputs(0)
+        quantise_flipped(1)
+        quantise_x2(0)
+        quantise_inputs(1)
+        for k in range(3):
+            unit(1, k)
+        mix(0)
+        regroup_x_pieces(gp_copy, "b", 2, 3, 4)
+        finish(0, nc.gpsimd)
+        regroup_x(nc.scalar.copy, "a", 2)
+        regroup_x(nc.scalar.copy, "b", 2, 0, 3 * P)
 
-        for i in range(BATCH):
-            nxt = i + 1
-            if i + LOOKAHEAD < BATCH:
-                load_batch(i + LOOKAHEAD)
-            if nxt < BATCH:
-                flip("a", nxt)
-            diffuse("a", i)
-            if nxt < BATCH:
-                quantise_flipped("a", nxt)
-            quantise_x2("a", i)
-            if nxt < BATCH:
-                flip("b", nxt)
-            diffuse("b", i)
-            if nxt < BATCH:
-                quantise_flipped("b", nxt)
-            quantise_x2("b", i)
-            if nxt < BATCH:
-                regroup_batch(nxt, (nc.scalar.copy, nc.scalar.copy, nc.scalar.copy))
-                quantise_inputs(nxt)
+        for i in range(1, BATCH):
+            if i + 4 < BATCH:
+                load_batch(i + 4)
+            diffuse_rest(i)
+            if i + 2 < BATCH:
+                flip_both(i + 2)
+                regroup_x(nc.scalar.copy, "0", i + 2)
+            if i + 1 < BATCH:
+                quantise_flipped(i + 1)
+                quantise_x2(i)
+                quantise_inputs(i + 1)
+                for k in range(3):
+                    unit(i + 1, k)
+            else:
+                quantise_x2_half(i, 1)
             mix(i)
+            if i + 2 < BATCH:
+                regroup_x_pieces(gp_copy, "b", i + 2, 3, 4)
+            finish(i, nc.gpsimd if i + 1 < BATCH else nc.vector)
+            if i + 2 < BATCH:
+                regroup_x(nc.scalar.copy, "a", i + 2)
+                regroup_x(nc.scalar.copy, "b", i + 2, 0, 3 * P)

@@ -240,14 +240,20 @@ def tile_dcgrucell_pc_t_kernel(tc, x_cand, x1_0, x1_1, support0, support1, W_c, 
                     stop=(k == 4),
                 )
 
-        def finish(b, eng):
+        def finish(b, eng, parts):
             cand = three.tile([P, NODES], F32, name="cand", tag="cand")
-            nc.scalar.activation(out=cand[:], in_=po_of[b][:], func=ACT.Tanh, bias=bias[:, 0:1], scale=1.0)
             res = three.tile([P, NODES], F32, name="res", tag="res")
-            eng.tensor_tensor(out=res[:], in0=hx_sb[:, b, :], in1=cand[:], op=ALU.subtract)
-            eng.tensor_tensor(out=res[:], in0=res[:], in1=u_sb[:, b, :], op=ALU.mult)
-            eng.tensor_tensor(out=res[:], in0=res[:], in1=cand[:], op=ALU.add)
-            nc.sync.dma_start(out=out[b], in_=res[:])
+            width = NODES // parts
+            cols = [slice(q * width, (q + 1) * width) for q in range(parts)]
+            for c in cols:
+                nc.scalar.activation(out=cand[:, c], in_=po_of[b][:, c], func=ACT.Tanh, bias=bias[:, 0:1], scale=1.0)
+            for c in cols:
+                eng.tensor_tensor(out=res[:, c], in0=hx_sb[:, b, c], in1=cand[:, c], op=ALU.subtract)
+            for c in cols:
+                eng.tensor_tensor(out=res[:, c], in0=res[:, c], in1=u_sb[:, b, c], op=ALU.mult)
+            for c in cols:
+                eng.tensor_tensor(out=res[:, c], in0=res[:, c], in1=cand[:, c], op=ALU.add)
+                nc.sync.dma_start(out=out[b][:, c], in_=res[:, c])
 
         def flip_both(k):
             flip("a", k)
@@ -311,7 +317,7 @@ def tile_dcgrucell_pc_t_kernel(tc, x_cand, x1_0, x1_1, support0, support1, W_c, 
             unit(1, k)
         mix(0)
         regroup_x_pieces(gp_copy, "b", 2, 3, 4)
-        finish(0, nc.gpsimd)
+        finish(0, nc.gpsimd, 1)
         regroup_x(nc.scalar.copy, "a", 2)
         regroup_x(nc.scalar.copy, "b", 2, 0, 3 * P)
 
@@ -333,7 +339,7 @@ def tile_dcgrucell_pc_t_kernel(tc, x_cand, x1_0, x1_1, support0, support1, W_c, 
             mix(i)
             if i + 2 < BATCH:
                 regroup_x_pieces(gp_copy, "b", i + 2, 3, 4)
-            finish(i, nc.gpsimd if i + 1 < BATCH else nc.vector)
+            finish(i, nc.gpsimd if i + 1 < BATCH else nc.vector, 1 if i + 1 < BATCH else 2)
             if i + 2 < BATCH:
                 regroup_x(nc.scalar.copy, "a", i + 2)
                 regroup_x(nc.scalar.copy, "b", i + 2, 0, 3 * P)

@@ -240,13 +240,22 @@ def tile_dcgrucell_pc_t_kernel(tc, x_cand, x1_0, x1_1, support0, support1, W_c, 
                     stop=(k == 4),
                 )
 
-        def finish(b, eng, parts):
-            cand = three.tile([P, NODES], F32, name="cand", tag="cand")
-            res = three.tile([P, NODES], F32, name="res", tag="res")
+        cand_of = {}
+
+        def column_parts(parts):
             width = NODES // parts
-            cols = [slice(q * width, (q + 1) * width) for q in range(parts)]
-            for c in cols:
+            return [slice(q * width, (q + 1) * width) for q in range(parts)]
+
+        def squash(b, parts):
+            cand = three.tile([P, NODES], F32, name="cand", tag="cand")
+            cand_of[b] = cand
+            for c in column_parts(parts):
                 nc.scalar.activation(out=cand[:, c], in_=po_of[b][:, c], func=ACT.Tanh, bias=bias[:, 0:1], scale=1.0)
+
+        def blend(b, eng, parts):
+            cand = cand_of[b]
+            res = three.tile([P, NODES], F32, name="res", tag="res")
+            cols = column_parts(parts)
             for c in cols:
                 eng.tensor_tensor(out=res[:, c], in0=hx_sb[:, b, c], in1=cand[:, c], op=ALU.subtract)
             for c in cols:
@@ -317,7 +326,8 @@ def tile_dcgrucell_pc_t_kernel(tc, x_cand, x1_0, x1_1, support0, support1, W_c, 
             unit(1, k)
         mix(0)
         regroup_x_pieces(gp_copy, "b", 2, 3, 4)
-        finish(0, nc.gpsimd, 1)
+        squash(0, 1)
+        blend(0, nc.gpsimd, 1)
         regroup_x(nc.scalar.copy, "a", 2)
         regroup_x(nc.scalar.copy, "b", 2, 0, 3 * P)
 
@@ -339,7 +349,15 @@ def tile_dcgrucell_pc_t_kernel(tc, x_cand, x1_0, x1_1, support0, support1, W_c, 
             mix(i)
             if i + 2 < BATCH:
                 regroup_x_pieces(gp_copy, "b", i + 2, 3, 4)
-            finish(i, nc.gpsimd if i + 1 < BATCH else nc.vector, 1 if i + 1 < BATCH else 2)
+            if i < BATCH - 2:
+                squash(i, 1)
+                blend(i, nc.gpsimd, 1)
+            elif i == BATCH - 2:
+                squash(i, 1)
+            else:
+                blend(i - 1, nc.vector, 2)
+                squash(i, 2)
+                blend(i, nc.vector, 2)
             if i + 2 < BATCH:
                 regroup_x(nc.scalar.copy, "a", i + 2)
                 regroup_x(nc.scalar.copy, "b", i + 2, 0, 3 * P)

@@ -21,6 +21,7 @@ W_TILE = PACK * NODES
 FLOPS = 2 * (2 * BATCH * CH * NODES * NODES) + 2 * BATCH * HID * 5 * CH * NODES
 
 MANUAL = True
+PRE = 4
 W_BLOCK = (0, 1, 3, 2, 4)
 
 
@@ -34,8 +35,7 @@ def tile_dcgrucell_pc_t_kernel(tc, x_cand, x1_0, x1_1, support0, support1, W_c, 
         two = ctx.enter_context(tc.tile_pool(name="two", bufs=2))
         three = ctx.enter_context(tc.tile_pool(name="three", bufs=3))
         ps_t = ctx.enter_context(tc.psum_pool(name="ps_t", bufs=4))
-        ps_x = ctx.enter_context(tc.psum_pool(name="ps_x", bufs=3))
-        ps_o = ctx.enter_context(tc.psum_pool(name="ps_o", bufs=1))
+        ps_x = ctx.enter_context(tc.psum_pool(name="ps_x", bufs=4))
 
         ident = const.tile([P, P], F32, name="ident")
         make_identity(nc, ident[:])
@@ -226,7 +226,7 @@ def tile_dcgrucell_pc_t_kernel(tc, x_cand, x1_0, x1_1, support0, support1, W_c, 
 
         def mix(b):
             codes, scales = hq[b]
-            po = ps_o.tile([P, NODES], F32, name="po", tag="po")
+            po = ps_t.tile([P, NODES], F32, name="po", tag="pt")
             po_of[b] = po
             for k in range(5):
                 wcols = slice(W_BLOCK[k] * HID, (W_BLOCK[k] + 1) * HID)
@@ -271,8 +271,8 @@ def tile_dcgrucell_pc_t_kernel(tc, x_cand, x1_0, x1_1, support0, support1, W_c, 
         def diffuse_rest(i):
             for k in range(8):
                 combine(i, k)
-                if k + 3 < 8:
-                    unit(i, k + 3)
+                if k + PRE < 8:
+                    unit(i, k + PRE)
                 if i == BATCH - 1 and k == 5:
                     quantise_x2_half(i, 0)
 
@@ -285,15 +285,13 @@ def tile_dcgrucell_pc_t_kernel(tc, x_cand, x1_0, x1_1, support0, support1, W_c, 
         quantise_support("s0")
         flip("b", 0)
         flip_support("s1")
-        for k in range(3):
+        for k in range(4):
             unit(0, k)
         regroup_x(nc.vector.tensor_copy, "b", 0)
         w_grp = const.tile([P, 5, HID, PACK], BF16, name="w_grp", align_bytes=64)
         for g in range(5):
             regroup(gp_copy, w_raw[:, g, :, :], w_grp[:, g, :, :])
-        combine(0, 0)
-        unit(0, 3)
-        for k in range(1, 4):
+        for k in range(4):
             combine(0, k)
         quantise_flipped_half("b", 0)
         quantise_support("s1")
@@ -301,15 +299,13 @@ def tile_dcgrucell_pc_t_kernel(tc, x_cand, x1_0, x1_1, support0, support1, W_c, 
         nc.vector.tensor_copy(out=bias[:], in_=bias_bf[:])
         flip("a", 1)
         regroup_x(nc.scalar.copy, "0", 1)
-        for k in range(4, 7):
-            unit(0, k)
         flip("b", 1)
+        for k in range(4, 8):
+            unit(0, k)
         regroup_x(nc.scalar.copy, "a", 1)
         regroup_x(nc.scalar.copy, "b", 1)
         quantise_inputs(0)
-        combine(0, 4)
-        unit(0, 7)
-        for k in range(5, 8):
+        for k in range(4, 8):
             combine(0, k)
         load_batch(4)
         flip_both(2)
@@ -322,9 +318,10 @@ def tile_dcgrucell_pc_t_kernel(tc, x_cand, x1_0, x1_1, support0, support1, W_c, 
         quantise_flipped(1)
         quantise_x2(0)
         quantise_inputs(1)
-        for k in range(3):
+        for k in range(PRE - 1):
             unit(1, k)
         mix(0)
+        unit(1, PRE - 1)
         regroup_x_pieces(gp_copy, "b", 2, 3, 4)
         squash(0, 1)
         blend(0, nc.gpsimd, 1)
@@ -342,11 +339,13 @@ def tile_dcgrucell_pc_t_kernel(tc, x_cand, x1_0, x1_1, support0, support1, W_c, 
                 quantise_flipped(i + 1)
                 quantise_x2(i)
                 quantise_inputs(i + 1)
-                for k in range(3):
+                for k in range(PRE - 1):
                     unit(i + 1, k)
             else:
                 quantise_x2_half(i, 1)
             mix(i)
+            if i + 1 < BATCH:
+                unit(i + 1, PRE - 1)
             if i + 2 < BATCH:
                 regroup_x_pieces(gp_copy, "b", i + 2, 3, 4)
             if i < BATCH - 2:

@@ -97,10 +97,10 @@ def tile_dcgrucell_pc_t_kernel(tc, x_cand, x1_0, x1_1, support0, support1, W_c, 
         def gp_copy(out, in_):
             nc.gpsimd.tensor_scalar(out=out, in0=in_, scalar1=1.0, scalar2=0.0, op0=ALU.mult, op1=ALU.add)
 
-        def regroup(copy_fn, src3, dst3):
+        def regroup(copy_fn, src3, dst3, run=4):
             copy_fn(
-                out=dst3.rearrange("p (c i) t -> p c t i", i=4),
-                in_=src3.rearrange("p t (c i) -> p c t i", i=4),
+                out=dst3.rearrange("p (c i) t -> p c t i", i=run),
+                in_=src3.rearrange("p t (c i) -> p c t i", i=run),
             )
 
         g1 = {}
@@ -147,7 +147,7 @@ def tile_dcgrucell_pc_t_kernel(tc, x_cand, x1_0, x1_1, support0, support1, W_c, 
         hq = {}
         SLOT = {"0": 0, "a": 1, "b": 2}
 
-        def regroup_x(copy_fn, s, b, n0=0, n1=NODES):
+        def regroup_x(copy_fn, s, b, n0=0, n1=NODES, run=4):
             if b not in hg:
                 g = three.tile([P, 3, W_TILE], BF16, name="hg", tag="hg", align_bytes=64)
                 hg[b] = g
@@ -155,6 +155,7 @@ def tile_dcgrucell_pc_t_kernel(tc, x_cand, x1_0, x1_1, support0, support1, W_c, 
                 copy_fn,
                 raw[(s, b)][:].rearrange("p (t n) -> p t n", t=PACK)[:, :, n0:n1],
                 hg[b][:, SLOT[s], PACK * n0 : PACK * n1].rearrange("p (n t) -> p n t", t=PACK),
+                run,
             )
 
         def regroup_x_pieces(copy_fn, s, b, first, last):
@@ -298,18 +299,18 @@ def tile_dcgrucell_pc_t_kernel(tc, x_cand, x1_0, x1_1, support0, support1, W_c, 
         bias = const.tile([P, 1], F32, name="bias")
         nc.vector.tensor_copy(out=bias[:], in_=bias_bf[:])
         flip("a", 1)
-        regroup_x(nc.scalar.copy, "0", 1)
+        regroup_x(nc.scalar.copy, "0", 1, run=2)
         flip("b", 1)
         for k in range(4, 8):
             unit(0, k)
-        regroup_x(nc.scalar.copy, "a", 1)
-        regroup_x(nc.scalar.copy, "b", 1)
+        regroup_x(nc.scalar.copy, "a", 1, run=2)
+        regroup_x(nc.scalar.copy, "b", 1, run=2)
         quantise_inputs(0)
         for k in range(4, 8):
             combine(0, k)
         load_batch(4)
         flip_both(2)
-        regroup_x(nc.scalar.copy, "0", 2)
+        regroup_x(nc.scalar.copy, "0", 2, run=2)
         w_codes = const.tile([P, 5 * HID], U32, name="w_codes", align_bytes=64)
         w_scales = const.tile([P, 5 * HID], U8, name="w_scales", align_bytes=64)
         w_flat = w_grp[:].rearrange("p g o j -> p (g o j)")
@@ -325,8 +326,8 @@ def tile_dcgrucell_pc_t_kernel(tc, x_cand, x1_0, x1_1, support0, support1, W_c, 
         regroup_x_pieces(gp_copy, "b", 2, 3, 4)
         squash(0, 1)
         blend(0, nc.gpsimd, 1)
-        regroup_x(nc.scalar.copy, "a", 2)
-        regroup_x(nc.scalar.copy, "b", 2, 0, 3 * P)
+        regroup_x(nc.scalar.copy, "a", 2, run=2)
+        regroup_x(nc.scalar.copy, "b", 2, 0, 3 * P, run=2)
 
         for i in range(1, BATCH):
             if i + 4 < BATCH:
@@ -334,7 +335,7 @@ def tile_dcgrucell_pc_t_kernel(tc, x_cand, x1_0, x1_1, support0, support1, W_c, 
             diffuse_rest(i)
             if i + 2 < BATCH:
                 flip_both(i + 2)
-                regroup_x(nc.scalar.copy, "0", i + 2)
+                regroup_x(nc.scalar.copy, "0", i + 2, run=2)
             if i + 1 < BATCH:
                 quantise_flipped(i + 1)
                 quantise_x2(i)
@@ -358,5 +359,5 @@ def tile_dcgrucell_pc_t_kernel(tc, x_cand, x1_0, x1_1, support0, support1, W_c, 
                 squash(i, 2)
                 blend(i, nc.vector, 2)
             if i + 2 < BATCH:
-                regroup_x(nc.scalar.copy, "a", i + 2)
-                regroup_x(nc.scalar.copy, "b", i + 2, 0, 3 * P)
+                regroup_x(nc.scalar.copy, "a", i + 2, run=2)
+                regroup_x(nc.scalar.copy, "b", i + 2, 0, 3 * P, run=2)

from contextlib import ExitStack

import concourse.mybir as mybir
from concourse.masks import make_identity

F32 = mybir.dt.float32
BF16 = mybir.dt.bfloat16
U32 = mybir.dt.uint32
U8 = mybir.dt.uint8
FP8X4 = mybir.dt.float8_e4m3fn_x4
ALU = mybir.AluOpType
ACT = mybir.ActivationFunctionType

P = 128
PACK = 4
BATCH = 8
CH = 512
NODES = 512
HID = 128
W_TILE = PACK * NODES
FLOPS = 2 * (2 * BATCH * CH * NODES * NODES) + 2 * BATCH * HID * 5 * CH * NODES

MANUAL = True
PRE = 4
W_BLOCK = (0, 1, 3, 2, 4)


def tile_dcgrucell_pc_t_kernel(tc, x_cand, x1_0, x1_1, support0, support1, W_c, b_c, u, hx, out):
    nc = tc.nc
    with ExitStack() as ctx:
        if MANUAL:
            ctx.enter_context(tc.manual_schedule())
        const = ctx.enter_context(tc.tile_pool(name="const", bufs=1))
        xin = ctx.enter_context(tc.tile_pool(name="xin", bufs=14))
        two = ctx.enter_context(tc.tile_pool(name="two", bufs=2))
        three = ctx.enter_context(tc.tile_pool(name="three", bufs=3))
        ps_t = ctx.enter_context(tc.psum_pool(name="ps_t", bufs=4))
        ps_x = ctx.enter_context(tc.psum_pool(name="ps_x", bufs=4))

        ident = const.tile([P, P], F32, name="ident")
        make_identity(nc, ident[:])

        raw = {}

        def load_x(key, src):
            t = xin.tile([P, W_TILE], BF16, name="xin", tag="xin")
            nc.sync.dma_start(out=t[:], in_=src.rearrange("(p j) n -> p (j n)", j=PACK))
            raw[key] = t

        def load_support(key, src):
            t = xin.tile([P, W_TILE], BF16, name="xin", tag="xin")
            nc.sync.dma_start(
                out=t[:].rearrange("p (t n) -> p t n", t=PACK),
                in_=src.rearrange("(t p) n -> p t n", p=P),
            )
            raw[key] = t

        def load_batch(b):
            load_x(("a", b), x1_0[b])
            load_x(("0", b), x_cand[b])
            load_x(("b", b), x1_1[b])

        load_x(("a", 0), x1_0[0])
        load_support("s0", support0)
        load_x(("0", 0), x_cand[0])
        load_x(("b", 0), x1_1[0])
        load_support("s1", support1)
        w_raw = const.tile([P, 5, PACK, HID], BF16, name="w_raw")
        nc.sync.dma_start(out=w_raw[:], in_=W_c.rearrange("(g p j) o -> p g j o", p=P, j=PACK))
        bias_bf = const.tile([P, 1], BF16, name="bias_bf")
        with nc.allow_non_contiguous_dma(reason="one bias value a partition"):
            nc.sync.dma_start(out=bias_bf[:], in_=b_c.rearrange("(p o) -> p o", o=1))
        load_batch(1)
        load_batch(2)
        u_sb = const.tile([P, BATCH, NODES], BF16, name="u_sb")
        nc.sync.dma_start(out=u_sb[:], in_=u.rearrange("b o n -> o b n"))
        hx_sb = const.tile([P, BATCH, NODES], BF16, name="hx_sb")
        nc.sync.dma_start(out=hx_sb[:], in_=hx.rearrange("b o n -> o b n"))
        load_batch(3)

        def transpose_words(src, dstw):
            srcw = src[:].bitcast(F32)
            for h in range(2):
                pt = ps_t.tile([P, 2, 256], F32, name="pt", tag="pt")
                for jj in range(2):
                    for uu in range(2):
                        col = (2 * h + jj) * 256 + uu * P
                        nc.tensor.transpose(pt[:, uu, jj * P : (jj + 1) * P], srcw[:, col : col + P], ident[:])
                nc.scalar.copy(
                    out=dstw[:, h * 512 : (h + 1) * 512].rearrange("p (c u) -> p c u", u=2),
                    in_=pt[:].rearrange("p u c -> p c u"),
                )

        def quantise(src, codes, scales):
            nc.vector.quantize_mx(out=codes.bitcast(FP8X4), scales=scales, in_=src)

        def gp_copy(out, in_):
            nc.gpsimd.tensor_scalar(out=out, in0=in_, scalar1=1.0, scalar2=0.0, op0=ALU.mult, op1=ALU.add)

        def regroup(copy_fn, src3, dst3, run=4):
            copy_fn(
                out=dst3.rearrange("p (c i) t -> p c t i", i=run),
                in_=src3.rearrange("p t (c i) -> p c t i", i=run),
            )

        g1 = {}
        c1 = {}
        SIDE = {"a": 0, "b": 1}

        def flip(s, b):
            if s == "a":
                g = two.tile([P, 2, W_TILE], BF16, name="g1", tag="g1", align_bytes=64)
                g1[b] = g
            transpose_words(raw[(s, b)], g1[b][:, SIDE[s], :].bitcast(F32))

        def alloc_c1(b):
            codes = two.tile([P, 2 * NODES], U32, name="c1", tag="c1", align_bytes=64)
            scales = two.tile([P, 2 * NODES], U8, name="s1", tag="s1", align_bytes=64)
            c1[b] = (codes, scales)

        def quantise_flipped_half(s, b):
            codes, scales = c1[b]
            cols = slice(SIDE[s] * NODES, (SIDE[s] + 1) * NODES)
            quantise(g1[b][:, SIDE[s], :], codes[:, cols], scales[:, cols])

        def quantise_flipped(b):
            alloc_c1(b)
            codes, scales = c1[b]
            quantise(g1[b][:].rearrange("p a k -> p (a k)"), codes[:], scales[:])

        sup = {}
        sup_g = {}

        def flip_support(key):
            g = two.tile([P, W_TILE], BF16, name="gs", tag="gs", align_bytes=64)
            transpose_words(raw[key], g[:].bitcast(F32))
            sup_g[key] = g

        def quantise_support(key):
            codes = const.tile([P, NODES], U32, name="c" + key, align_bytes=64)
            scales = const.tile([P, NODES], U8, name="p" + key, align_bytes=64)
            quantise(sup_g[key][:], codes[:], scales[:])
            sup[key] = (codes, scales)

        hg = {}
        x2g = {}
        hq = {}
        SLOT = {"0": 0, "a": 1, "b": 2}

        def regroup_x(copy_fn, s, b, n0=0, n1=NODES, run=4):
            if b not in hg:
                g = three.tile([P, 3, W_TILE], BF16, name="hg", tag="hg", align_bytes=64)
                hg[b] = g
            regroup(
                copy_fn,
                raw[(s, b)][:].rearrange("p (t n) -> p t n", t=PACK)[:, :, n0:n1],
                hg[b][:, SLOT[s], PACK * n0 : PACK * n1].rearrange("p (n t) -> p n t", t=PACK),
                run,
            )

        def regroup_x_pieces(copy_fn, s, b, first, last):
            for q in range(first, last):
                regroup_x(copy_fn, s, b, q * P, (q + 1) * P)

        def quantise_inputs(b):
            codes = two.tile([P, 5, NODES], U32, name="hc", tag="hc", align_bytes=64)
            scales = two.tile([P, 5, NODES], U8, name="hs", tag="hs", align_bytes=64)
            hq[b] = (codes, scales)
            quantise(
                hg[b][:, 0:2, :].rearrange("p a k -> p (a k)"),
                codes[:, 0:2, :].rearrange("p a k -> p (a k)"),
                scales[:, 0:2, :].rearrange("p a k -> p (a k)"),
            )
            quantise(hg[b][:, 2, :], codes[:, 2, :], scales[:, 2, :])

        px_of = {}

        def unit(b, k):
            si = k // 4
            mq = k % 4
            codes, scales = c1[b]
            scodes, sscales = sup["s%d" % si]
            px = ps_x.tile([P, PACK, P], F32, name="px", tag="px")
            px_of[(b, k)] = px
            mcols = slice(mq * P, (mq + 1) * P)
            for j in range(PACK):
                ccols = slice(si * NODES + j * P, si * NODES + (j + 1) * P)
                nc.tensor.matmul_mx(
                    out=px[:, j, :],
                    lhsT=codes[:, ccols].bitcast(FP8X4),
                    lhsT_scale=scales[:, ccols],
                    rhs=scodes[:, mcols].bitcast(FP8X4),
                    rhs_scale=sscales[:, mcols],
                    start=True,
                    stop=True,
                )

        def combine(b, k):
            si = k // 4
            mq = k % 4
            if k == 0:
                x2 = two.tile([P, 2, W_TILE], BF16, name="x2g", tag="x2g", align_bytes=64)
                x2g[b] = x2
            gcols = slice(mq * 512, (mq + 1) * 512)
            nc.vector.scalar_tensor_tensor(
                out=x2g[b][:, si, gcols].rearrange("p (m j) -> p m j", j=PACK),
                in0=px_of[(b, k)][:].rearrange("p j m -> p m j"),
                scalar=2.0,
                in1=hg[b][:, 0, gcols].rearrange("p (m j) -> p m j", j=PACK),
                op0=ALU.mult,
                op1=ALU.subtract,
            )

        def quantise_x2(b):
            codes, scales = hq[b]
            quantise(
                x2g[b][:].rearrange("p a k -> p (a k)"),
                codes[:, 3:5, :].rearrange("p a k -> p (a k)"),
                scales[:, 3:5, :].rearrange("p a k -> p (a k)"),
            )

        def quantise_x2_half(b, si):
            codes, scales = hq[b]
            quantise(x2g[b][:, si, :], codes[:, 3 + si, :], scales[:, 3 + si, :])

        po_of = {}

        def mix(b):
            codes, scales = hq[b]
            po = ps_t.tile([P, NODES], F32, name="po", tag="pt")
            po_of[b] = po
            for k in range(5):
                wcols = slice(W_BLOCK[k] * HID, (W_BLOCK[k] + 1) * HID)
                nc.tensor.matmul_mx(
                    out=po[:],
                    lhsT=w_codes[:, wcols].bitcast(FP8X4),
                    lhsT_scale=w_scales[:, wcols],
                    rhs=codes[:, k, :].bitcast(FP8X4),
                    rhs_scale=scales[:, k, :],
                    start=(k == 0),
                    stop=(k == 4),
                )

        cand_of = {}

        def column_parts(parts):
            width = NODES // parts
            return [slice(q * width, (q + 1) * width) for q in range(parts)]

        def squash(b, parts):
            cand = three.tile([P, NODES], F32, name="cand", tag="cand")
            cand_of[b] = cand
            for c in column_parts(parts):
                nc.scalar.activation(out=cand[:, c], in_=po_of[b][:, c], func=ACT.Tanh, bias=bias[:, 0:1], scale=1.0)

        def blend(b, eng, parts):
            cand = cand_of[b]
            res = three.tile([P, NODES], F32, name="res", tag="res")
            cols = column_parts(parts)
            for c in cols:
                eng.tensor_tensor(out=res[:, c], in0=hx_sb[:, b, c], in1=cand[:, c], op=ALU.subtract)
            for c in cols:
                eng.tensor_tensor(out=res[:, c], in0=res[:, c], in1=u_sb[:, b, c], op=ALU.mult)
            for c in cols:
                eng.tensor_tensor(out=res[:, c], in0=res[:, c], in1=cand[:, c], op=ALU.add)
                nc.sync.dma_start(out=out[b][:, c], in_=res[:, c])

        def flip_both(k):
            flip("a", k)
            flip("b", k)

        def diffuse_rest(i):
            for k in range(8):
                combine(i, k)
                if k + PRE < 8:
                    unit(i, k + PRE)
                if i == BATCH - 1 and k == 5:
                    quantise_x2_half(i, 0)

        flip("a", 0)
        flip_support("s0")
        regroup_x(nc.vector.tensor_copy, "a", 0)
        alloc_c1(0)
        quantise_flipped_half("a", 0)
        regroup_x(nc.vector.tensor_copy, "0", 0)
        quantise_support("s0")
        flip("b", 0)
        flip_support("s1")
        for k in range(4):
            unit(0, k)
        regroup_x(nc.vector.tensor_copy, "b", 0)
        w_grp = const.tile([P, 5, HID, PACK], BF16, name="w_grp", align_bytes=64)
        for g in range(5):
            regroup(gp_copy, w_raw[:, g, :, :], w_grp[:, g, :, :])
        for k in range(4):
            combine(0, k)
        quantise_flipped_half("b", 0)
        quantise_support("s1")
        bias = const.tile([P, 1], F32, name="bias")
        nc.vector.tensor_copy(out=bias[:], in_=bias_bf[:])
        flip("a", 1)
        regroup_x(nc.scalar.copy, "0", 1, run=2)
        flip("b", 1)
        for k in range(4, 8):
            unit(0, k)
        regroup_x(nc.scalar.copy, "a", 1, run=2)
        regroup_x(nc.scalar.copy, "b", 1, run=2)
        quantise_inputs(0)
        for k in range(4, 8):
            combine(0, k)
        load_batch(4)
        flip_both(2)
        regroup_x(nc.scalar.copy, "0", 2, run=2)
        w_codes = const.tile([P, 5 * HID], U32, name="w_codes", align_bytes=64)
        w_scales = const.tile([P, 5 * HID], U8, name="w_scales", align_bytes=64)
        w_flat = w_grp[:].rearrange("p g o j -> p (g o j)")
        quantise(w_flat[:, 0:2048], w_codes[:, 0:512], w_scales[:, 0:512])
        quantise(w_flat[:, 2048:2560], w_codes[:, 512:640], w_scales[:, 512:640])
        quantise_flipped(1)
        quantise_x2(0)
        quantise_inputs(1)
        for k in range(PRE - 1):
            unit(1, k)
        mix(0)
        unit(1, PRE - 1)
        regroup_x_pieces(gp_copy, "b", 2, 3, 4)
        squash(0, 1)
        blend(0, nc.gpsimd, 1)
        regroup_x(nc.scalar.copy, "a", 2, run=2)
        regroup_x(nc.scalar.copy, "b", 2, 0, 3 * P, run=2)

        for i in range(1, BATCH):
            if i + 4 < BATCH:
                load_batch(i + 4)
            diffuse_rest(i)
            if i + 2 < BATCH:
                flip_both(i + 2)
                regroup_x(nc.scalar.copy, "0", i + 2, run=2)
            if i + 1 < BATCH:
                quantise_flipped(i + 1)
                quantise_x2(i)
                quantise_inputs(i + 1)
                for k in range(PRE - 1):
                    unit(i + 1, k)
            else:
                quantise_x2_half(i, 1)
            mix(i)
            if i + 1 < BATCH:
                unit(i + 1, PRE - 1)
            if i + 2 < BATCH:
                regroup_x_pieces(gp_copy, "b", i + 2, 3, 4)
            if i < BATCH - 2:
                squash(i, 1)
                blend(i, nc.gpsimd, 1)
            elif i == BATCH - 2:
                squash(i, 1)
            else:
                blend(i - 1, nc.vector, 2)
                squash(i, 2)
                blend(i, nc.vector, 2)
            if i + 2 < BATCH:
                regroup_x(nc.scalar.copy, "a", i + 2, run=2)
                regroup_x(nc.scalar.copy, "b", i + 2, 0, 3 * P, run=2)
